import numpy as np
import ml_dtypes


def mxq(x, axis, fmt="e4m3"):
    dtype, down = {"e4m3": (ml_dtypes.float8_e4m3fn, 7), "e5m2": (ml_dtypes.float8_e5m2, 14)}[fmt]
    v = np.moveaxis(np.asarray(x, np.float32).astype(ml_dtypes.bfloat16).astype(np.float64), axis, -1)
    blocks = v.reshape(v.shape[:-1] + (-1, 32))
    amax = np.abs(blocks).max(-1, keepdims=True)
    byte = np.maximum(np.where(amax > 0, np.frexp(amax)[1] - 1 + 127, 0) - down, 1)
    scale = np.exp2(byte - 127.0)
    codes = (blocks / scale).astype(np.float32).astype(dtype).astype(np.float64)
    return np.moveaxis((codes * scale).reshape(v.shape), -1, axis)


WIDE = False


def mx_kscale(k):
    if not WIDE:
        return np.ones(k)
    levels = np.array([10, -10, 5, -5, 0])
    if k % 512:
        return np.exp2(np.random.permutation(np.resize(levels, k // 32))).repeat(32)
    a = np.empty((k // 512, 16))
    for p in range(k // 512):
        a[p, :8] = np.random.permutation(np.resize(levels, 8))
        for g in range(8):
            far = levels[np.abs(levels - a[p, g]) >= 10]
            a[p, g + 8] = far[np.random.randint(len(far))]
    return np.exp2(a.ravel()).repeat(32)


BF16 = ml_dtypes.bfloat16


def bf(x):
    return np.asarray(x, np.float32).astype(BF16)


def f64(x):
    return np.asarray(x).astype(np.float64)


B, X, N, OS = 8192, 512, 640, 128
H = N - OS


def setup_inputs():
    s, t = mx_kscale(X), mx_kscale(H)
    std0 = np.sqrt(2.0 / X)
    std1 = np.sqrt(2.0 / (X + H))
    row_scale = np.concatenate([std0 * t, np.full(OS, std1)])
    bias_scale = np.concatenate([t, np.ones(OS)])
    return {"x": bf(np.random.standard_normal((B, X)) * s),
            "w0": bf(np.random.standard_normal((N, X)) * row_scale[:, None] / s),
            "w1": bf(np.random.standard_normal((OS, H)) * std1 / t),
            "biases": bf(np.random.random(N) * bias_scale)}


def reference(x, w0, w1, biases):
    n = w0.shape[0]
    os_ = w1.shape[0]
    z = (mxq(f64(x), 1, "e4m3") @ mxq(f64(w0), 1, "e4m3").T) + f64(biases)
    h = np.maximum(z[:, : n - os_], 0.0)
    return z[:, n - os_:] + (mxq(h, 1, "e4m3") @ mxq(f64(w1), 1, "e4m3").T)

@@ -1,0 +1,275 @@
+from contextlib import ExitStack
+
+import concourse.mybir as mybir
+from concourse.masks import make_identity
+
+BF16 = mybir.dt.bfloat16
+F32 = mybir.dt.float32
+U32 = mybir.dt.uint32
+U8 = mybir.dt.uint8
+FP8X4 = mybir.dt.float8_e4m3fn_x4
+
+P = 128
+PACK = 4
+HALVES = 2
+BATCH = 8192
+INPUTS = 512
+HIDDEN = 512
+OUTS = 128
+ROUND = 512
+TILES = ROUND // P
+ROUNDS = BATCH // ROUND
+W_TILES = 6
+VECTOR_ROWS = 320
+
+OUT_W0 = slice(HIDDEN, HIDDEN + OUTS)
+W1 = slice(HIDDEN + OUTS, HIDDEN + 2 * OUTS)
+
+FLOPS = 2 * BATCH * INPUTS * (HIDDEN + OUTS) + 2 * BATCH * HIDDEN * OUTS
+
+
+def transpose_two_tiles(nc, banks, identity, rows, first):
+    bank = banks.tile([P, 2, HALVES, P], F32, tag="bank")
+    for j in range(2):
+        words = rows[:, first + j, :].bitcast(F32)
+        for u in range(HALVES):
+            nc.tensor.transpose(
+                out=bank[:, j, u, :],
+                in_=words[:, u : HALVES * P : HALVES],
+                identity=identity[:],
+            )
+    return bank
+
+
+def words_side_by_side(bank):
+    return bank[:].rearrange("p j u r -> p j r u")
+
+
+def copy_four_tiles_out(nc, banks, grouped):
+    nc.scalar.copy(out=grouped[:, 0:2, :, :].bitcast(F32), in_=words_side_by_side(banks[0]))
+    nc.vector.tensor_copy(
+        out=grouped[:, 2:4, :, :].bitcast(F32), in_=words_side_by_side(banks[1])
+    )
+
+
+def tile_spn_t_kernel(tc, x, w0, w1, biases, out):
+    nc = tc.nc
+    with ExitStack() as stack:
+        stack.enter_context(tc.manual_schedule())
+        keep = stack.enter_context(tc.tile_pool(name="keep", bufs=1))
+        stream = stack.enter_context(tc.tile_pool(name="stream", bufs=3))
+        x_mx_pool = stack.enter_context(tc.tile_pool(name="x_mx", bufs=6))
+        transposed_psum = stack.enter_context(tc.psum_pool(name="transposed", bufs=2))
+        hidden_psum = stack.enter_context(tc.psum_pool(name="hidden", bufs=PACK))
+        result_psum = stack.enter_context(tc.psum_pool(name="result", bufs=2))
+
+        w_rows = keep.tile([P, W_TILES, INPUTS], BF16)
+        nc.sync.dma_start(
+            out=w_rows[:, 0:PACK, :],
+            in_=w0[0:HIDDEN, :].rearrange("(m t) k -> m t k", t=PACK),
+        )
+        x_rows = []
+
+        def load_x(r):
+            rows = keep.tile([P, TILES, INPUTS], BF16, name="x_rows_%d" % r)
+            nc.sync.dma_start(
+                out=rows[:],
+                in_=x[r * ROUND : (r + 1) * ROUND, :].rearrange("(p j) k -> p j k", j=TILES),
+            )
+            x_rows.append(rows)
+
+        load_x(0)
+        nc.sync.dma_start(out=w_rows[:, PACK, :], in_=w0[HIDDEN : HIDDEN + OUTS, :])
+        nc.sync.dma_start(out=w_rows[:, PACK + 1, :], in_=w1[:, :])
+        for r in range(1, ROUNDS):
+            load_x(r)
+        bias_hidden = keep.tile([P, PACK], BF16)
+        nc.scalar.dma_start(
+            out=bias_hidden[:],
+            in_=biases[0:HIDDEN].rearrange("(m t) -> m t", t=PACK),
+        )
+        bias_out = keep.tile([P, OUTS], BF16)
+        nc.scalar.dma_start(
+            out=bias_out[:], in_=biases[HIDDEN : HIDDEN + OUTS].partition_broadcast(P)
+        )
+
+        identity = keep.tile([P, P], F32)
+        make_identity(nc, identity[:])
+
+        w_grouped = keep.tile([P, W_TILES, P, PACK], BF16, align_bytes=64)
+        w_codes = keep.tile([P, W_TILES * P], U32, align_bytes=64)
+        w_scales = keep.tile([P, W_TILES * P], U8, align_bytes=64)
+
+        def quantise_w(first, last):
+            columns = slice(first * P, last * P)
+            nc.vector.quantize_mx(
+                out=w_codes[:, columns].bitcast(FP8X4),
+                scales=w_scales[:, columns],
+                in_=w_grouped[:, first:last, :, :].rearrange("p j r t -> p (j r t)"),
+            )
+
+        x_banks = {}
+        x_grouped = {}
+        x_mx = {}
+        h_banks = {}
+        h_planes = {}
+        h_grouped = {}
+        h_mx = {}
+        result_banks = {}
+
+        def transpose_x(r):
+            x_banks[r] = [
+                transpose_two_tiles(nc, transposed_psum, identity, x_rows[r], first)
+                for first in range(0, TILES, 2)
+            ]
+
+        def copy_x_out(r):
+            grouped = stream.tile([P, TILES, P, PACK], BF16, align_bytes=64, name="x_grouped")
+            copy_four_tiles_out(nc, x_banks[r], grouped)
+            x_grouped[r] = grouped
+
+        def quantise_x(r):
+            codes = x_mx_pool.tile([P, ROUND], U32, align_bytes=64, name="x_codes")
+            scales = x_mx_pool.tile([P, ROUND], U8, align_bytes=64, name="x_scales")
+            nc.vector.quantize_mx(
+                out=codes[:].bitcast(FP8X4),
+                scales=scales[:],
+                in_=x_grouped[r][:].rearrange("p j r t -> p (j r t)"),
+            )
+            x_mx[r] = (codes, scales)
+
+        def hidden_matmuls(r):
+            codes, scales = x_mx[r]
+            h_banks[r] = []
+            for t in range(PACK):
+                nodes = slice(t * P, (t + 1) * P)
+                bank = hidden_psum.tile([P, ROUND], F32, tag="bank")
+                nc.tensor.matmul_mx(
+                    out=bank[:],
+                    lhsT=w_codes[:, nodes].bitcast(FP8X4),
+                    lhsT_scale=w_scales[:, nodes],
+                    rhs=codes[:].bitcast(FP8X4),
+                    rhs_scale=scales[:],
+                    start=True,
+                    stop=True,
+                )
+                h_banks[r].append(bank)
+
+        def relu_out(r):
+            planes = stream.tile([P, PACK, ROUND], BF16, name="h_planes")
+            for t, bank in enumerate(h_banks[r]):
+                nc.scalar.activation(
+                    out=planes[:, t, :],
+                    in_=bank[:],
+                    func=mybir.ActivationFunctionType.Relu,
+                    bias=bias_hidden[:, t : t + 1],
+                    scale=1.0,
+                )
+            h_planes[r] = planes
+
+        def regroup_h(r):
+            planes = h_planes[r]
+            grouped = stream.tile([P, ROUND, PACK], BF16, align_bytes=64, name="h_grouped")
+            nc.vector.tensor_copy(
+                out=grouped[:, 0:VECTOR_ROWS, :].rearrange("p (c i) t -> p c t i", i=4),
+                in_=planes[:, :, 0:VECTOR_ROWS].rearrange("p t (c i) -> p c t i", i=4),
+            )
+            nc.gpsimd.tensor_scalar(
+                out=grouped[:, VECTOR_ROWS:ROUND, :],
+                in0=planes[:, :, VECTOR_ROWS:ROUND].rearrange("p t c -> p c t"),
+                scalar1=1.0,
+                scalar2=0.0,
+                op0=mybir.AluOpType.mult,
+                op1=mybir.AluOpType.add,
+            )
+            h_grouped[r] = grouped
+
+        def quantise_h(r):
+            codes = stream.tile([P, ROUND], U32, align_bytes=64, name="h_codes")
+            scales = stream.tile([P, ROUND], U8, align_bytes=64, name="h_scales")
+            nc.vector.quantize_mx(
+                out=codes[:].bitcast(FP8X4),
+                scales=scales[:],
+                in_=h_grouped[r][:].rearrange("p c t -> p (c t)"),
+            )
+            h_mx[r] = (codes, scales)
+
+        def output_matmuls(r):
+            x_codes, x_scales = x_mx[r]
+            h_codes, h_scales = h_mx[r]
+            bank = result_psum.tile([P, TILES, OUTS], F32, tag="bank")
+            for j in range(TILES):
+                rows = slice(j * P, (j + 1) * P)
+                nc.tensor.matmul_mx(
+                    out=bank[:, j, :],
+                    lhsT=x_codes[:, rows].bitcast(FP8X4),
+                    lhsT_scale=x_scales[:, rows],
+                    rhs=w_codes[:, OUT_W0].bitcast(FP8X4),
+                    rhs_scale=w_scales[:, OUT_W0],
+                    start=True,
+                    stop=False,
+                )
+                nc.tensor.matmul_mx(
+                    out=bank[:, j, :],
+                    lhsT=h_codes[:, rows].bitcast(FP8X4),
+                    lhsT_scale=h_scales[:, rows],
+                    rhs=w_codes[:, W1].bitcast(FP8X4),
+                    rhs_scale=w_scales[:, W1],
+                    start=False,
+                    stop=True,
+                )
+            result_banks[r] = bank
+
+        def add_bias_and_store(r):
+            result = stream.tile([P, TILES, OUTS], F32, name="result")
+            nc.vector.tensor_tensor(
+                out=result[:],
+                in0=result_banks[r][:],
+                in1=bias_out[:].unsqueeze(1).to_broadcast([P, TILES, OUTS]),
+                op=mybir.AluOpType.add,
+            )
+            nc.sync.dma_start(
+                out=out[r * ROUND : (r + 1) * ROUND, :].rearrange("(p j) o -> p j o", j=TILES),
+                in_=result[:],
+            )
+
+        def live(r):
+            return 0 <= r < ROUNDS
+
+        hidden_w_banks = [
+            transpose_two_tiles(nc, hidden_psum, identity, w_rows, first)
+            for first in range(0, PACK, 2)
+        ]
+        transpose_x(0)
+        output_w_bank = transpose_two_tiles(nc, result_psum, identity, w_rows, PACK)
+        copy_four_tiles_out(nc, hidden_w_banks, w_grouped[:, 0:PACK, :, :])
+        copy_x_out(0)
+        quantise_w(0, PACK)
+        quantise_x(0)
+        nc.scalar.copy(
+            out=w_grouped[:, PACK:W_TILES, :, :].bitcast(F32),
+            in_=words_side_by_side(output_w_bank),
+        )
+        quantise_w(PACK, W_TILES)
+        transpose_x(1)
+        hidden_matmuls(0)
+
+        for s in range(1, ROUNDS + 4):
+            if live(s):
+                copy_x_out(s)
+            if live(s - 1):
+                relu_out(s - 1)
+            if live(s - 3):
+                quantise_h(s - 3)
+            if live(s):
+                quantise_x(s)
+            if live(s - 2):
+                regroup_h(s - 2)
+            if live(s - 4):
+                output_matmuls(s - 4)
+            if live(s + 1):
+                transpose_x(s + 1)
+            if live(s):
+                hidden_matmuls(s)
+            if live(s - 4):
+                add_bias_and_store(s - 4)

@@ -20,7 +20,6 @@ ROUND = 512
 TILES = ROUND // P
 ROUNDS = BATCH // ROUND
 W_TILES = 6
-VECTOR_ROWS = 320
 
 OUT_W0 = slice(HIDDEN, HIDDEN + OUTS)
 W1 = slice(HIDDEN + OUTS, HIDDEN + 2 * OUTS)
@@ -171,16 +170,8 @@ def tile_spn_t_kernel(tc, x, w0, w1, biases, out):
             planes = h_planes[r]
             grouped = stream.tile([P, ROUND, PACK], BF16, align_bytes=64, name="h_grouped")
             nc.vector.tensor_copy(
-                out=grouped[:, 0:VECTOR_ROWS, :].rearrange("p (c i) t -> p c t i", i=4),
-                in_=planes[:, :, 0:VECTOR_ROWS].rearrange("p t (c i) -> p c t i", i=4),
-            )
-            nc.gpsimd.tensor_scalar(
-                out=grouped[:, VECTOR_ROWS:ROUND, :],
-                in0=planes[:, :, VECTOR_ROWS:ROUND].rearrange("p t c -> p c t"),
-                scalar1=1.0,
-                scalar2=0.0,
-                op0=mybir.AluOpType.mult,
-                op1=mybir.AluOpType.add,
+                out=grouped[:].rearrange("p (c i) t -> p c t i", i=4),
+                in_=planes[:].rearrange("p t (c i) -> p c t i", i=4),
             )
             h_grouped[r] = grouped
 

@@ -19,6 +19,7 @@ OUTS = 128
 ROUND = 512
 TILES = ROUND // P
 ROUNDS = BATCH // ROUND
+VECTOR_COPIES_EVERY = 4
 W_TILES = 6
 
 OUT_W0 = slice(HIDDEN, HIDDEN + OUTS)
@@ -44,13 +45,6 @@ def words_side_by_side(bank):
     return bank[:].rearrange("p j u r -> p j r u")
 
 
-def copy_four_tiles_out(nc, banks, grouped):
-    nc.scalar.copy(out=grouped[:, 0:2, :, :].bitcast(F32), in_=words_side_by_side(banks[0]))
-    nc.vector.tensor_copy(
-        out=grouped[:, 2:4, :, :].bitcast(F32), in_=words_side_by_side(banks[1])
-    )
-
-
 def tile_spn_t_kernel(tc, x, w0, w1, biases, out):
     nc = tc.nc
     with ExitStack() as stack:
@@ -62,11 +56,6 @@ def tile_spn_t_kernel(tc, x, w0, w1, biases, out):
         hidden_psum = stack.enter_context(tc.psum_pool(name="hidden", bufs=PACK))
         result_psum = stack.enter_context(tc.psum_pool(name="result", bufs=2))
 
-        w_rows = keep.tile([P, W_TILES, INPUTS], BF16)
-        nc.sync.dma_start(
-            out=w_rows[:, 0:PACK, :],
-            in_=w0[0:HIDDEN, :].rearrange("(m t) k -> m t k", t=PACK),
-        )
         x_rows = []
 
         def load_x(r):
@@ -77,10 +66,18 @@ def tile_spn_t_kernel(tc, x, w0, w1, biases, out):
             )
             x_rows.append(rows)
 
+        w_rows = keep.tile([P, W_TILES, INPUTS], BF16)
+        hidden_rows = w0[0:HIDDEN, :].rearrange("(m t) k -> m t k", t=PACK)
         load_x(0)
+        for first in range(0, PACK, 2):
+            nc.sync.dma_start(
+                out=w_rows[:, first : first + 2, :], in_=hidden_rows[:, first : first + 2, :]
+            )
+        load_x(1)
+        load_x(2)
         nc.sync.dma_start(out=w_rows[:, PACK, :], in_=w0[HIDDEN : HIDDEN + OUTS, :])
         nc.sync.dma_start(out=w_rows[:, PACK + 1, :], in_=w1[:, :])
-        for r in range(1, ROUNDS):
+        for r in range(3, ROUNDS):
             load_x(r)
         bias_hidden = keep.tile([P, PACK], BF16)
         nc.scalar.dma_start(
@@ -124,8 +121,14 @@ def tile_spn_t_kernel(tc, x, w0, w1, biases, out):
 
         def copy_x_out(r):
             grouped = stream.tile([P, TILES, P, PACK], BF16, align_bytes=64, name="x_grouped")
-            copy_four_tiles_out(nc, x_banks[r], grouped)
             x_grouped[r] = grouped
+            words = grouped[:].bitcast(F32)
+            first, second = x_banks[r]
+            nc.scalar.copy(out=words[:, 0:2, :, :], in_=words_side_by_side(first))
+            if r % VECTOR_COPIES_EVERY == 0:
+                nc.vector.tensor_copy(out=words[:, 2:4, :, :], in_=words_side_by_side(second))
+            else:
+                nc.scalar.copy(out=words[:, 2:4, :, :], in_=words_side_by_side(second))
 
         def quantise_x(r):
             codes = x_mx_pool.tile([P, ROUND], U32, align_bytes=64, name="x_codes")
@@ -227,40 +230,42 @@ def tile_spn_t_kernel(tc, x, w0, w1, biases, out):
         def live(r):
             return 0 <= r < ROUNDS
 
+        transpose_x(0)
         hidden_w_banks = [
             transpose_two_tiles(nc, hidden_psum, identity, w_rows, first)
             for first in range(0, PACK, 2)
         ]
-        transpose_x(0)
-        output_w_bank = transpose_two_tiles(nc, result_psum, identity, w_rows, PACK)
-        copy_four_tiles_out(nc, hidden_w_banks, w_grouped[:, 0:PACK, :, :])
         copy_x_out(0)
-        quantise_w(0, PACK)
+        w_words = w_grouped[:].bitcast(F32)
+        nc.scalar.copy(out=w_words[:, 0:2, :, :], in_=words_side_by_side(hidden_w_banks[0]))
+        nc.vector.tensor_copy(out=w_words[:, 2:4, :, :], in_=words_side_by_side(hidden_w_banks[1]))
         quantise_x(0)
-        nc.scalar.copy(
-            out=w_grouped[:, PACK:W_TILES, :, :].bitcast(F32),
-            in_=words_side_by_side(output_w_bank),
-        )
-        quantise_w(PACK, W_TILES)
-        transpose_x(1)
-        hidden_matmuls(0)
+        quantise_w(0, PACK)
 
-        for s in range(1, ROUNDS + 4):
-            if live(s):
-                copy_x_out(s)
-            if live(s - 1):
-                relu_out(s - 1)
-            if live(s - 3):
-                quantise_h(s - 3)
-            if live(s):
-                quantise_x(s)
-            if live(s - 2):
-                regroup_h(s - 2)
-            if live(s - 4):
-                output_matmuls(s - 4)
+        for s in range(ROUNDS + 3):
             if live(s + 1):
                 transpose_x(s + 1)
+            if s == 0:
+                output_w_bank = transpose_two_tiles(nc, result_psum, identity, w_rows, PACK)
+            if live(s - 3):
+                output_matmuls(s - 3)
             if live(s):
                 hidden_matmuls(s)
-            if live(s - 4):
-                add_bias_and_store(s - 4)
+            if live(s + 1):
+                copy_x_out(s + 1)
+            if s == 0:
+                nc.scalar.copy(
+                    out=w_words[:, PACK:W_TILES, :, :], in_=words_side_by_side(output_w_bank)
+                )
+            if live(s):
+                relu_out(s)
+            if live(s - 2):
+                quantise_h(s - 2)
+            if live(s - 1):
+                regroup_h(s - 1)
+            if s == 0:
+                quantise_w(PACK, W_TILES)
+            if live(s + 1):
+                quantise_x(s + 1)
+            if live(s - 3):
+                add_bias_and_store(s - 3)

@@ -19,7 +19,10 @@ OUTS = 128
 ROUND = 512
 TILES = ROUND // P
 ROUNDS = BATCH // ROUND
-VECTOR_COPIES_EVERY = 4
+DIRECT_ROWS = 128
+PLANE_ROWS = ROUND - DIRECT_ROWS
+GPSIMD_ROWS = 208
+VECTOR_ROWS = PLANE_ROWS - GPSIMD_ROWS
 W_TILES = 6
 
 OUT_W0 = slice(HIDDEN, HIDDEN + OUTS)
@@ -52,9 +55,11 @@ def tile_spn_t_kernel(tc, x, w0, w1, biases, out):
         keep = stack.enter_context(tc.tile_pool(name="keep", bufs=1))
         stream = stack.enter_context(tc.tile_pool(name="stream", bufs=3))
         x_mx_pool = stack.enter_context(tc.tile_pool(name="x_mx", bufs=6))
+        grouped_pool = stack.enter_context(tc.tile_pool(name="grouped", bufs=3))
         transposed_psum = stack.enter_context(tc.psum_pool(name="transposed", bufs=2))
         hidden_psum = stack.enter_context(tc.psum_pool(name="hidden", bufs=PACK))
-        result_psum = stack.enter_context(tc.psum_pool(name="result", bufs=2))
+        direct_psum = stack.enter_context(tc.psum_pool(name="direct", bufs=1))
+        result_psum = stack.enter_context(tc.psum_pool(name="result", bufs=1))
 
         x_rows = []
 
@@ -108,6 +113,7 @@ def tile_spn_t_kernel(tc, x, w0, w1, biases, out):
         x_grouped = {}
         x_mx = {}
         h_banks = {}
+        direct_banks = {}
         h_planes = {}
         h_grouped = {}
         h_mx = {}
@@ -120,12 +126,12 @@ def tile_spn_t_kernel(tc, x, w0, w1, biases, out):
             ]
 
         def copy_x_out(r):
-            grouped = stream.tile([P, TILES, P, PACK], BF16, align_bytes=64, name="x_grouped")
+            grouped = grouped_pool.tile([P, TILES, P, PACK], BF16, align_bytes=64, tag="grouped")
             x_grouped[r] = grouped
             words = grouped[:].bitcast(F32)
             first, second = x_banks[r]
             nc.scalar.copy(out=words[:, 0:2, :, :], in_=words_side_by_side(first))
-            if r % VECTOR_COPIES_EVERY == 0:
+            if r == 0:
                 nc.vector.tensor_copy(out=words[:, 2:4, :, :], in_=words_side_by_side(second))
             else:
                 nc.scalar.copy(out=words[:, 2:4, :, :], in_=words_side_by_side(second))
@@ -140,29 +146,39 @@ def tile_spn_t_kernel(tc, x, w0, w1, biases, out):
             )
             x_mx[r] = (codes, scales)
 
-        def hidden_matmuls(r):
+        def hidden_pass(r, t, out, rows):
             codes, scales = x_mx[r]
+            nodes = slice(t * P, (t + 1) * P)
+            nc.tensor.matmul_mx(
+                out=out,
+                lhsT=w_codes[:, nodes].bitcast(FP8X4),
+                lhsT_scale=w_scales[:, nodes],
+                rhs=codes[:, rows].bitcast(FP8X4),
+                rhs_scale=scales[:, rows],
+                start=True,
+                stop=True,
+            )
+
+        def hidden_matmuls(r):
             h_banks[r] = []
             for t in range(PACK):
-                nodes = slice(t * P, (t + 1) * P)
                 bank = hidden_psum.tile([P, ROUND], F32, tag="bank")
-                nc.tensor.matmul_mx(
-                    out=bank[:],
-                    lhsT=w_codes[:, nodes].bitcast(FP8X4),
-                    lhsT_scale=w_scales[:, nodes],
-                    rhs=codes[:].bitcast(FP8X4),
-                    rhs_scale=scales[:],
-                    start=True,
-                    stop=True,
-                )
+                for rows in (slice(0, 256), slice(256, PLANE_ROWS)):
+                    hidden_pass(r, t, bank[:, rows], rows)
                 h_banks[r].append(bank)
 
+        def direct_matmuls(r):
+            bank = direct_psum.tile([P, PACK, DIRECT_ROWS], F32, name="direct_bank")
+            for t in range(PACK):
+                hidden_pass(r, t, bank[:, t, :], slice(PLANE_ROWS, ROUND))
+            direct_banks[r] = bank
+
         def relu_out(r):
-            planes = stream.tile([P, PACK, ROUND], BF16, name="h_planes")
+            planes = stream.tile([P, PACK, PLANE_ROWS], BF16, name="h_planes")
             for t, bank in enumerate(h_banks[r]):
                 nc.scalar.activation(
                     out=planes[:, t, :],
-                    in_=bank[:],
+                    in_=bank[:, 0:PLANE_ROWS],
                     func=mybir.ActivationFunctionType.Relu,
                     bias=bias_hidden[:, t : t + 1],
                     scale=1.0,
@@ -171,12 +187,33 @@ def tile_spn_t_kernel(tc, x, w0, w1, biases, out):
 
         def regroup_h(r):
             planes = h_planes[r]
-            grouped = stream.tile([P, ROUND, PACK], BF16, align_bytes=64, name="h_grouped")
+            grouped = h_grouped[r]
             nc.vector.tensor_copy(
-                out=grouped[:].rearrange("p (c i) t -> p c t i", i=4),
-                in_=planes[:].rearrange("p t (c i) -> p c t i", i=4),
+                out=grouped[:, 0:VECTOR_ROWS, :].rearrange("p (c i) t -> p c t i", i=4),
+                in_=planes[:, :, 0:VECTOR_ROWS].rearrange("p t (c i) -> p c t i", i=4),
             )
+            nc.gpsimd.tensor_scalar(
+                out=grouped[:, VECTOR_ROWS:PLANE_ROWS, :],
+                in0=planes[:, :, VECTOR_ROWS:PLANE_ROWS].rearrange("p t c -> p c t"),
+                scalar1=1.0,
+                scalar2=0.0,
+                op0=mybir.AluOpType.mult,
+                op1=mybir.AluOpType.add,
+            )
+
+        def add_direct_bias(r):
+            grouped = grouped_pool.tile([P, ROUND, PACK], BF16, align_bytes=64, tag="grouped")
             h_grouped[r] = grouped
+            nc.vector.tensor_tensor(
+                out=grouped[:, PLANE_ROWS:ROUND, :],
+                in0=direct_banks[r][:].rearrange("p t c -> p c t"),
+                in1=bias_hidden[:].unsqueeze(1).to_broadcast([P, DIRECT_ROWS, PACK]),
+                op=mybir.AluOpType.add,
+            )
+
+        def relu_direct(r):
+            values = h_grouped[r][:, PLANE_ROWS:ROUND, :]
+            nc.vector.tensor_scalar_max(out=values, in0=values, scalar1=0.0)
 
         def quantise_h(r):
             codes = stream.tile([P, ROUND], U32, align_bytes=64, name="h_codes")
@@ -235,6 +272,7 @@ def tile_spn_t_kernel(tc, x, w0, w1, biases, out):
             transpose_two_tiles(nc, hidden_psum, identity, w_rows, first)
             for first in range(0, PACK, 2)
         ]
+        transpose_x(1)
         copy_x_out(0)
         w_words = w_grouped[:].bitcast(F32)
         nc.scalar.copy(out=w_words[:, 0:2, :, :], in_=words_side_by_side(hidden_w_banks[0]))
@@ -243,12 +281,18 @@ def tile_spn_t_kernel(tc, x, w0, w1, biases, out):
         quantise_w(0, PACK)
 
         for s in range(ROUNDS + 3):
-            if live(s + 1):
+            if 0 < s < ROUNDS:
+                quantise_x(s)
+            if live(s - 2):
+                quantise_h(s - 2)
+            if 1 < s + 1 < ROUNDS:
                 transpose_x(s + 1)
-            if s == 0:
-                output_w_bank = transpose_two_tiles(nc, result_psum, identity, w_rows, PACK)
+            if live(s - 1):
+                direct_matmuls(s - 1)
             if live(s - 3):
                 output_matmuls(s - 3)
+            if s == 0:
+                output_w_bank = transpose_two_tiles(nc, result_psum, identity, w_rows, PACK)
             if live(s):
                 hidden_matmuls(s)
             if live(s + 1):
@@ -259,13 +303,13 @@ def tile_spn_t_kernel(tc, x, w0, w1, biases, out):
                 )
             if live(s):
                 relu_out(s)
-            if live(s - 2):
-                quantise_h(s - 2)
+            if live(s - 1):
+                add_direct_bias(s - 1)
+            if live(s - 3):
+                add_bias_and_store(s - 3)
             if live(s - 1):
                 regroup_h(s - 1)
             if s == 0:
                 quantise_w(PACK, W_TILES)
-            if live(s + 1):
-                quantise_x(s + 1)
-            if live(s - 3):
-                add_bias_and_store(s - 3)
+            if live(s - 1):
+                relu_direct(s - 1)

@@ -21,7 +21,8 @@ TILES = ROUND // P
 ROUNDS = BATCH // ROUND
 DIRECT_ROWS = 128
 PLANE_ROWS = ROUND - DIRECT_ROWS
-GPSIMD_ROWS = 208
+GPSIMD_ROWS = 192
+LASTV = 64
 VECTOR_ROWS = PLANE_ROWS - GPSIMD_ROWS
 W_TILES = 6
 
@@ -55,6 +56,7 @@ def tile_spn_t_kernel(tc, x, w0, w1, biases, out):
         keep = stack.enter_context(tc.tile_pool(name="keep", bufs=1))
         stream = stack.enter_context(tc.tile_pool(name="stream", bufs=3))
         x_mx_pool = stack.enter_context(tc.tile_pool(name="x_mx", bufs=6))
+        result_pool = stack.enter_context(tc.tile_pool(name="results", bufs=6))
         grouped_pool = stack.enter_context(tc.tile_pool(name="grouped", bufs=3))
         transposed_psum = stack.enter_context(tc.psum_pool(name="transposed", bufs=2))
         hidden_psum = stack.enter_context(tc.psum_pool(name="hidden", bufs=PACK))
@@ -73,7 +75,13 @@ def tile_spn_t_kernel(tc, x, w0, w1, biases, out):
 
         w_rows = keep.tile([P, W_TILES, INPUTS], BF16)
         hidden_rows = w0[0:HIDDEN, :].rearrange("(m t) k -> m t k", t=PACK)
-        load_x(0)
+        rows = keep.tile([P, TILES, INPUTS], BF16, name="x_rows_0")
+        round_0 = x[0:ROUND, :].rearrange("(p j) k -> p j k", j=TILES)
+        for first in range(0, TILES, 2):
+            nc.sync.dma_start(
+                out=rows[:, first : first + 2, :], in_=round_0[:, first : first + 2, :]
+            )
+        x_rows.append(rows)
         for first in range(0, PACK, 2):
             nc.sync.dma_start(
                 out=w_rows[:, first : first + 2, :], in_=hidden_rows[:, first : first + 2, :]
@@ -117,7 +125,6 @@ def tile_spn_t_kernel(tc, x, w0, w1, biases, out):
         h_planes = {}
         h_grouped = {}
         h_mx = {}
-        result_banks = {}
 
         def transpose_x(r):
             x_banks[r] = [
@@ -185,27 +192,38 @@ def tile_spn_t_kernel(tc, x, w0, w1, biases, out):
                 )
             h_planes[r] = planes
 
-        def regroup_h(r):
-            planes = h_planes[r]
-            grouped = h_grouped[r]
-            nc.vector.tensor_copy(
-                out=grouped[:, 0:VECTOR_ROWS, :].rearrange("p (c i) t -> p c t i", i=4),
-                in_=planes[:, :, 0:VECTOR_ROWS].rearrange("p t (c i) -> p c t i", i=4),
-            )
+        def grouped_h(r):
+            if r not in h_grouped:
+                grouped = grouped_pool.tile([P, ROUND, PACK], BF16, align_bytes=64, tag="grouped")
+                h_grouped[r] = grouped
+            return h_grouped[r]
+
+        def regroup_on_vector(r, first, last):
+            if first < last:
+                nc.vector.tensor_copy(
+                    out=grouped_h(r)[:, first:last, :].rearrange("p (c i) t -> p c t i", i=4),
+                    in_=h_planes[r][:, :, first:last].rearrange("p t (c i) -> p c t i", i=4),
+                )
+
+        def regroup_on_gpsimd(r, first, last):
             nc.gpsimd.tensor_scalar(
-                out=grouped[:, VECTOR_ROWS:PLANE_ROWS, :],
-                in0=planes[:, :, VECTOR_ROWS:PLANE_ROWS].rearrange("p t c -> p c t"),
+                out=grouped_h(r)[:, first:last, :],
+                in0=h_planes[r][:, :, first:last].rearrange("p t c -> p c t"),
                 scalar1=1.0,
                 scalar2=0.0,
                 op0=mybir.AluOpType.mult,
                 op1=mybir.AluOpType.add,
             )
 
+        def regroup_on_scalar(r, first, last):
+            nc.scalar.copy(
+                out=grouped_h(r)[:, first:last, :].rearrange("p (c i) t -> p c t i", i=4),
+                in_=h_planes[r][:, :, first:last].rearrange("p t (c i) -> p c t i", i=4),
+            )
+
         def add_direct_bias(r):
-            grouped = grouped_pool.tile([P, ROUND, PACK], BF16, align_bytes=64, tag="grouped")
-            h_grouped[r] = grouped
             nc.vector.tensor_tensor(
-                out=grouped[:, PLANE_ROWS:ROUND, :],
+                out=grouped_h(r)[:, PLANE_ROWS:ROUND, :],
                 in0=direct_banks[r][:].rearrange("p t c -> p c t"),
                 in1=bias_hidden[:].unsqueeze(1).to_broadcast([P, DIRECT_ROWS, PACK]),
                 op=mybir.AluOpType.add,
@@ -225,11 +243,11 @@ def tile_spn_t_kernel(tc, x, w0, w1, biases, out):
             )
             h_mx[r] = (codes, scales)
 
-        def output_matmuls(r):
+        def output_matmuls(r, banks, tiles=range(TILES)):
             x_codes, x_scales = x_mx[r]
             h_codes, h_scales = h_mx[r]
-            bank = result_psum.tile([P, TILES, OUTS], F32, tag="bank")
-            for j in range(TILES):
+            bank = banks.tile([P, TILES, OUTS], F32, tag="bank")
+            for j in tiles:
                 rows = slice(j * P, (j + 1) * P)
                 nc.tensor.matmul_mx(
                     out=bank[:, j, :],
@@ -249,20 +267,19 @@ def tile_spn_t_kernel(tc, x, w0, w1, biases, out):
                     start=False,
                     stop=True,
                 )
-            result_banks[r] = bank
+            return bank
 
-        def add_bias_and_store(r):
-            result = stream.tile([P, TILES, OUTS], F32, name="result")
+        def add_bias_and_store(r, bank, tiles=slice(0, TILES)):
+            count = tiles.stop - tiles.start
+            result = result_pool.tile([P, TILES, OUTS], F32, name="result")
             nc.vector.tensor_tensor(
-                out=result[:],
-                in0=result_banks[r][:],
-                in1=bias_out[:].unsqueeze(1).to_broadcast([P, TILES, OUTS]),
+                out=result[:, tiles, :],
+                in0=bank[:, tiles, :],
+                in1=bias_out[:].unsqueeze(1).to_broadcast([P, count, OUTS]),
                 op=mybir.AluOpType.add,
             )
-            nc.sync.dma_start(
-                out=out[r * ROUND : (r + 1) * ROUND, :].rearrange("(p j) o -> p j o", j=TILES),
-                in_=result[:],
-            )
+            rows = out[r * ROUND : (r + 1) * ROUND, :].rearrange("(p j) o -> p j o", j=TILES)
+            nc.sync.dma_start(out=rows[:, tiles, :], in_=result[:, tiles, :])
 
         def live(r):
             return 0 <= r < ROUNDS
@@ -275,41 +292,67 @@ def tile_spn_t_kernel(tc, x, w0, w1, biases, out):
         transpose_x(1)
         copy_x_out(0)
         w_words = w_grouped[:].bitcast(F32)
-        nc.scalar.copy(out=w_words[:, 0:2, :, :], in_=words_side_by_side(hidden_w_banks[0]))
-        nc.vector.tensor_copy(out=w_words[:, 2:4, :, :], in_=words_side_by_side(hidden_w_banks[1]))
+        for first, bank in zip(range(0, PACK, 2), hidden_w_banks):
+            nc.scalar.copy(
+                out=w_words[:, first : first + 2, :, :], in_=words_side_by_side(bank)
+            )
         quantise_x(0)
-        quantise_w(0, PACK)
+        quantise_w(0, 2)
+        quantise_w(2, PACK)
 
-        for s in range(ROUNDS + 3):
-            if 0 < s < ROUNDS:
+        for s in range(ROUNDS):
+            if s > 0:
                 quantise_x(s)
-            if live(s - 2):
+            if s >= 2:
                 quantise_h(s - 2)
             if 1 < s + 1 < ROUNDS:
                 transpose_x(s + 1)
-            if live(s - 1):
-                direct_matmuls(s - 1)
-            if live(s - 3):
-                output_matmuls(s - 3)
-            if s == 0:
+            if s == 1:
                 output_w_bank = transpose_two_tiles(nc, result_psum, identity, w_rows, PACK)
-            if live(s):
-                hidden_matmuls(s)
-            if live(s + 1):
-                copy_x_out(s + 1)
+            if s >= 2:
+                direct_matmuls(s - 1)
+            if s >= 3:
+                result_bank = output_matmuls(s - 3, result_psum)
+            hidden_matmuls(s)
             if s == 0:
+                direct_matmuls(s)
+            if s + 1 < ROUNDS:
+                copy_x_out(s + 1)
+            else:
+                regroup_on_scalar(s - 1, VECTOR_ROWS, PLANE_ROWS)
+            if s == 1:
                 nc.scalar.copy(
                     out=w_words[:, PACK:W_TILES, :, :], in_=words_side_by_side(output_w_bank)
                 )
-            if live(s):
-                relu_out(s)
-            if live(s - 1):
+            relu_out(s)
+            if s >= 1:
                 add_direct_bias(s - 1)
-            if live(s - 3):
-                add_bias_and_store(s - 3)
-            if live(s - 1):
-                regroup_h(s - 1)
-            if s == 0:
+            if s >= 3:
+                add_bias_and_store(s - 3, result_bank)
+            if s >= 1:
+                if s - 1 < 2:
+                    regroup_on_vector(s - 1, 0, PLANE_ROWS)
+                else:
+                    regroup_on_vector(s - 1, 0, VECTOR_ROWS)
+                    if s + 1 < ROUNDS:
+                        regroup_on_gpsimd(s - 1, VECTOR_ROWS, PLANE_ROWS)
+            if s == 2:
                 quantise_w(PACK, W_TILES)
-            if live(s - 1):
+            if s >= 1:
                 relu_direct(s - 1)
+
+        last = ROUNDS - 1
+        quantise_h(last - 1)
+        direct_matmuls(last)
+        bank_13 = output_matmuls(last - 2, result_psum)
+        bank_14 = output_matmuls(last - 1, hidden_psum)
+        regroup_on_scalar(last, LASTV, PLANE_ROWS)
+        add_direct_bias(last)
+        regroup_on_vector(last, 0, LASTV)
+        relu_direct(last)
+        add_bias_and_store(last - 2, bank_13)
+        quantise_h(last)
+        add_bias_and_store(last - 1, bank_14)
+        for first in (0, 2):
+            bank = output_matmuls(last, hidden_psum, range(first, first + 2))
+            add_bias_and_store(last, bank, slice(first, first + 2))

@@ -86,21 +86,23 @@ def tile_spn_t_kernel(tc, x, w0, w1, biases, out):
             nc.sync.dma_start(
                 out=w_rows[:, first : first + 2, :], in_=hidden_rows[:, first : first + 2, :]
             )
+        bias_hidden = keep.tile([P, PACK], BF16)
+        nc.sync.dma_start(
+            out=bias_hidden[:],
+            in_=biases[0:HIDDEN].rearrange("(m t) -> m t", t=PACK),
+        )
         load_x(1)
         load_x(2)
         nc.sync.dma_start(out=w_rows[:, PACK, :], in_=w0[HIDDEN : HIDDEN + OUTS, :])
         nc.sync.dma_start(out=w_rows[:, PACK + 1, :], in_=w1[:, :])
-        for r in range(3, ROUNDS):
+        for r in range(3, 6):
             load_x(r)
-        bias_hidden = keep.tile([P, PACK], BF16)
-        nc.scalar.dma_start(
-            out=bias_hidden[:],
-            in_=biases[0:HIDDEN].rearrange("(m t) -> m t", t=PACK),
-        )
         bias_out = keep.tile([P, OUTS], BF16)
-        nc.scalar.dma_start(
+        nc.sync.dma_start(
             out=bias_out[:], in_=biases[HIDDEN : HIDDEN + OUTS].partition_broadcast(P)
         )
+        for r in range(6, ROUNDS):
+            load_x(r)
 
         identity = keep.tile([P, P], F32)
         make_identity(nc, identity[:])

from contextlib import ExitStack

import concourse.mybir as mybir
from concourse.masks import make_identity

BF16 = mybir.dt.bfloat16
F32 = mybir.dt.float32
U32 = mybir.dt.uint32
U8 = mybir.dt.uint8
FP8X4 = mybir.dt.float8_e4m3fn_x4

P = 128
PACK = 4
HALVES = 2
BATCH = 8192
INPUTS = 512
HIDDEN = 512
OUTS = 128
ROUND = 512
TILES = ROUND // P
ROUNDS = BATCH // ROUND
DIRECT_ROWS = 128
PLANE_ROWS = ROUND - DIRECT_ROWS
GPSIMD_ROWS = 192
LASTV = 64
VECTOR_ROWS = PLANE_ROWS - GPSIMD_ROWS
W_TILES = 6

OUT_W0 = slice(HIDDEN, HIDDEN + OUTS)
W1 = slice(HIDDEN + OUTS, HIDDEN + 2 * OUTS)

FLOPS = 2 * BATCH * INPUTS * (HIDDEN + OUTS) + 2 * BATCH * HIDDEN * OUTS


def transpose_two_tiles(nc, banks, identity, rows, first):
    bank = banks.tile([P, 2, HALVES, P], F32, tag="bank")
    for j in range(2):
        words = rows[:, first + j, :].bitcast(F32)
        for u in range(HALVES):
            nc.tensor.transpose(
                out=bank[:, j, u, :],
                in_=words[:, u : HALVES * P : HALVES],
                identity=identity[:],
            )
    return bank


def words_side_by_side(bank):
    return bank[:].rearrange("p j u r -> p j r u")


def tile_spn_t_kernel(tc, x, w0, w1, biases, out):
    nc = tc.nc
    with ExitStack() as stack:
        stack.enter_context(tc.manual_schedule())
        keep = stack.enter_context(tc.tile_pool(name="keep", bufs=1))
        stream = stack.enter_context(tc.tile_pool(name="stream", bufs=3))
        x_mx_pool = stack.enter_context(tc.tile_pool(name="x_mx", bufs=6))
        result_pool = stack.enter_context(tc.tile_pool(name="results", bufs=6))
        grouped_pool = stack.enter_context(tc.tile_pool(name="grouped", bufs=3))
        transposed_psum = stack.enter_context(tc.psum_pool(name="transposed", bufs=2))
        hidden_psum = stack.enter_context(tc.psum_pool(name="hidden", bufs=PACK))
        direct_psum = stack.enter_context(tc.psum_pool(name="direct", bufs=1))
        result_psum = stack.enter_context(tc.psum_pool(name="result", bufs=1))

        x_rows = []

        def load_x(r):
            rows = keep.tile([P, TILES, INPUTS], BF16, name="x_rows_%d" % r)
            nc.sync.dma_start(
                out=rows[:],
                in_=x[r * ROUND : (r + 1) * ROUND, :].rearrange("(p j) k -> p j k", j=TILES),
            )
            x_rows.append(rows)

        w_rows = keep.tile([P, W_TILES, INPUTS], BF16)
        hidden_rows = w0[0:HIDDEN, :].rearrange("(m t) k -> m t k", t=PACK)
        rows = keep.tile([P, TILES, INPUTS], BF16, name="x_rows_0")
        round_0 = x[0:ROUND, :].rearrange("(p j) k -> p j k", j=TILES)
        for first in range(0, TILES, 2):
            nc.sync.dma_start(
                out=rows[:, first : first + 2, :], in_=round_0[:, first : first + 2, :]
            )
        x_rows.append(rows)
        for first in range(0, PACK, 2):
            nc.sync.dma_start(
                out=w_rows[:, first : first + 2, :], in_=hidden_rows[:, first : first + 2, :]
            )
        bias_hidden = keep.tile([P, PACK], BF16)
        nc.sync.dma_start(
            out=bias_hidden[:],
            in_=biases[0:HIDDEN].rearrange("(m t) -> m t", t=PACK),
        )
        load_x(1)
        load_x(2)
        nc.sync.dma_start(out=w_rows[:, PACK, :], in_=w0[HIDDEN : HIDDEN + OUTS, :])
        nc.sync.dma_start(out=w_rows[:, PACK + 1, :], in_=w1[:, :])
        for r in range(3, 6):
            load_x(r)
        bias_out = keep.tile([P, OUTS], BF16)
        nc.sync.dma_start(
            out=bias_out[:], in_=biases[HIDDEN : HIDDEN + OUTS].partition_broadcast(P)
        )
        for r in range(6, ROUNDS):
            load_x(r)

        identity = keep.tile([P, P], F32)
        make_identity(nc, identity[:])

        w_grouped = keep.tile([P, W_TILES, P, PACK], BF16, align_bytes=64)
        w_codes = keep.tile([P, W_TILES * P], U32, align_bytes=64)
        w_scales = keep.tile([P, W_TILES * P], U8, align_bytes=64)

        def quantise_w(first, last):
            columns = slice(first * P, last * P)
            nc.vector.quantize_mx(
                out=w_codes[:, columns].bitcast(FP8X4),
                scales=w_scales[:, columns],
                in_=w_grouped[:, first:last, :, :].rearrange("p j r t -> p (j r t)"),
            )

        x_banks = {}
        x_grouped = {}
        x_mx = {}
        h_banks = {}
        direct_banks = {}
        h_planes = {}
        h_grouped = {}
        h_mx = {}

        def transpose_x(r):
            x_banks[r] = [
                transpose_two_tiles(nc, transposed_psum, identity, x_rows[r], first)
                for first in range(0, TILES, 2)
            ]

        def copy_x_out(r):
            grouped = grouped_pool.tile([P, TILES, P, PACK], BF16, align_bytes=64, tag="grouped")
            x_grouped[r] = grouped
            words = grouped[:].bitcast(F32)
            first, second = x_banks[r]
            nc.scalar.copy(out=words[:, 0:2, :, :], in_=words_side_by_side(first))
            if r == 0:
                nc.vector.tensor_copy(out=words[:, 2:4, :, :], in_=words_side_by_side(second))
            else:
                nc.scalar.copy(out=words[:, 2:4, :, :], in_=words_side_by_side(second))

        def quantise_x(r):
            codes = x_mx_pool.tile([P, ROUND], U32, align_bytes=64, name="x_codes")
            scales = x_mx_pool.tile([P, ROUND], U8, align_bytes=64, name="x_scales")
            nc.vector.quantize_mx(
                out=codes[:].bitcast(FP8X4),
                scales=scales[:],
                in_=x_grouped[r][:].rearrange("p j r t -> p (j r t)"),
            )
            x_mx[r] = (codes, scales)

        def hidden_pass(r, t, out, rows):
            codes, scales = x_mx[r]
            nodes = slice(t * P, (t + 1) * P)
            nc.tensor.matmul_mx(
                out=out,
                lhsT=w_codes[:, nodes].bitcast(FP8X4),
                lhsT_scale=w_scales[:, nodes],
                rhs=codes[:, rows].bitcast(FP8X4),
                rhs_scale=scales[:, rows],
                start=True,
                stop=True,
            )

        def hidden_matmuls(r):
            h_banks[r] = []
            for t in range(PACK):
                bank = hidden_psum.tile([P, ROUND], F32, tag="bank")
                for rows in (slice(0, 256), slice(256, PLANE_ROWS)):
                    hidden_pass(r, t, bank[:, rows], rows)
                h_banks[r].append(bank)

        def direct_matmuls(r):
            bank = direct_psum.tile([P, PACK, DIRECT_ROWS], F32, name="direct_bank")
            for t in range(PACK):
                hidden_pass(r, t, bank[:, t, :], slice(PLANE_ROWS, ROUND))
            direct_banks[r] = bank

        def relu_out(r):
            planes = stream.tile([P, PACK, PLANE_ROWS], BF16, name="h_planes")
            for t, bank in enumerate(h_banks[r]):
                nc.scalar.activation(
                    out=planes[:, t, :],
                    in_=bank[:, 0:PLANE_ROWS],
                    func=mybir.ActivationFunctionType.Relu,
                    bias=bias_hidden[:, t : t + 1],
                    scale=1.0,
                )
            h_planes[r] = planes

        def grouped_h(r):
            if r not in h_grouped:
                grouped = grouped_pool.tile([P, ROUND, PACK], BF16, align_bytes=64, tag="grouped")
                h_grouped[r] = grouped
            return h_grouped[r]

        def regroup_on_vector(r, first, last):
            if first < last:
                nc.vector.tensor_copy(
                    out=grouped_h(r)[:, first:last, :].rearrange("p (c i) t -> p c t i", i=4),
                    in_=h_planes[r][:, :, first:last].rearrange("p t (c i) -> p c t i", i=4),
                )

        def regroup_on_gpsimd(r, first, last):
            nc.gpsimd.tensor_scalar(
                out=grouped_h(r)[:, first:last, :],
                in0=h_planes[r][:, :, first:last].rearrange("p t c -> p c t"),
                scalar1=1.0,
                scalar2=0.0,
                op0=mybir.AluOpType.mult,
                op1=mybir.AluOpType.add,
            )

        def regroup_on_scalar(r, first, last):
            nc.scalar.copy(
                out=grouped_h(r)[:, first:last, :].rearrange("p (c i) t -> p c t i", i=4),
                in_=h_planes[r][:, :, first:last].rearrange("p t (c i) -> p c t i", i=4),
            )

        def add_direct_bias(r):
            nc.vector.tensor_tensor(
                out=grouped_h(r)[:, PLANE_ROWS:ROUND, :],
                in0=direct_banks[r][:].rearrange("p t c -> p c t"),
                in1=bias_hidden[:].unsqueeze(1).to_broadcast([P, DIRECT_ROWS, PACK]),
                op=mybir.AluOpType.add,
            )

        def relu_direct(r):
            values = h_grouped[r][:, PLANE_ROWS:ROUND, :]
            nc.vector.tensor_scalar_max(out=values, in0=values, scalar1=0.0)

        def quantise_h(r):
            codes = stream.tile([P, ROUND], U32, align_bytes=64, name="h_codes")
            scales = stream.tile([P, ROUND], U8, align_bytes=64, name="h_scales")
            nc.vector.quantize_mx(
                out=codes[:].bitcast(FP8X4),
                scales=scales[:],
                in_=h_grouped[r][:].rearrange("p c t -> p (c t)"),
            )
            h_mx[r] = (codes, scales)

        def output_matmuls(r, banks, tiles=range(TILES)):
            x_codes, x_scales = x_mx[r]
            h_codes, h_scales = h_mx[r]
            bank = banks.tile([P, TILES, OUTS], F32, tag="bank")
            for j in tiles:
                rows = slice(j * P, (j + 1) * P)
                nc.tensor.matmul_mx(
                    out=bank[:, j, :],
                    lhsT=x_codes[:, rows].bitcast(FP8X4),
                    lhsT_scale=x_scales[:, rows],
                    rhs=w_codes[:, OUT_W0].bitcast(FP8X4),
                    rhs_scale=w_scales[:, OUT_W0],
                    start=True,
                    stop=False,
                )
                nc.tensor.matmul_mx(
                    out=bank[:, j, :],
                    lhsT=h_codes[:, rows].bitcast(FP8X4),
                    lhsT_scale=h_scales[:, rows],
                    rhs=w_codes[:, W1].bitcast(FP8X4),
                    rhs_scale=w_scales[:, W1],
                    start=False,
                    stop=True,
                )
            return bank

        def add_bias_and_store(r, bank, tiles=slice(0, TILES)):
            count = tiles.stop - tiles.start
            result = result_pool.tile([P, TILES, OUTS], F32, name="result")
            nc.vector.tensor_tensor(
                out=result[:, tiles, :],
                in0=bank[:, tiles, :],
                in1=bias_out[:].unsqueeze(1).to_broadcast([P, count, OUTS]),
                op=mybir.AluOpType.add,
            )
            rows = out[r * ROUND : (r + 1) * ROUND, :].rearrange("(p j) o -> p j o", j=TILES)
            nc.sync.dma_start(out=rows[:, tiles, :], in_=result[:, tiles, :])

        def live(r):
            return 0 <= r < ROUNDS

        transpose_x(0)
        hidden_w_banks = [
            transpose_two_tiles(nc, hidden_psum, identity, w_rows, first)
            for first in range(0, PACK, 2)
        ]
        transpose_x(1)
        copy_x_out(0)
        w_words = w_grouped[:].bitcast(F32)
        for first, bank in zip(range(0, PACK, 2), hidden_w_banks):
            nc.scalar.copy(
                out=w_words[:, first : first + 2, :, :], in_=words_side_by_side(bank)
            )
        quantise_x(0)
        quantise_w(0, 2)
        quantise_w(2, PACK)

        for s in range(ROUNDS):
            if s > 0:
                quantise_x(s)
            if s >= 2:
                quantise_h(s - 2)
            if 1 < s + 1 < ROUNDS:
                transpose_x(s + 1)
            if s == 1:
                output_w_bank = transpose_two_tiles(nc, result_psum, identity, w_rows, PACK)
            if s >= 2:
                direct_matmuls(s - 1)
            if s >= 3:
                result_bank = output_matmuls(s - 3, result_psum)
            hidden_matmuls(s)
            if s == 0:
                direct_matmuls(s)
            if s + 1 < ROUNDS:
                copy_x_out(s + 1)
            else:
                regroup_on_scalar(s - 1, VECTOR_ROWS, PLANE_ROWS)
            if s == 1:
                nc.scalar.copy(
                    out=w_words[:, PACK:W_TILES, :, :], in_=words_side_by_side(output_w_bank)
                )
            relu_out(s)
            if s >= 1:
                add_direct_bias(s - 1)
            if s >= 3:
                add_bias_and_store(s - 3, result_bank)
            if s >= 1:
                if s - 1 < 2:
                    regroup_on_vector(s - 1, 0, PLANE_ROWS)
                else:
                    regroup_on_vector(s - 1, 0, VECTOR_ROWS)
                    if s + 1 < ROUNDS:
                        regroup_on_gpsimd(s - 1, VECTOR_ROWS, PLANE_ROWS)
            if s == 2:
                quantise_w(PACK, W_TILES)
            if s >= 1:
                relu_direct(s - 1)

        last = ROUNDS - 1
        quantise_h(last - 1)
        direct_matmuls(last)
        bank_13 = output_matmuls(last - 2, result_psum)
        bank_14 = output_matmuls(last - 1, hidden_psum)
        regroup_on_scalar(last, LASTV, PLANE_ROWS)
        add_direct_bias(last)
        regroup_on_vector(last, 0, LASTV)
        relu_direct(last)
        add_bias_and_store(last - 2, bank_13)
        quantise_h(last)
        add_bias_and_store(last - 1, bank_14)
        for first in (0, 2):
            bank = output_matmuls(last, hidden_psum, range(first, first + 2))
            add_bias_and_store(last, bank, slice(first, first + 2))
